import numpy as np
import ml_dtypes


def mxq(x, axis, fmt="e4m3"):
    dtype, down = {"e4m3": (ml_dtypes.float8_e4m3fn, 7), "e5m2": (ml_dtypes.float8_e5m2, 14)}[fmt]
    v = np.moveaxis(np.asarray(x, np.float32).astype(ml_dtypes.bfloat16).astype(np.float64), axis, -1)
    blocks = v.reshape(v.shape[:-1] + (-1, 32))
    amax = np.abs(blocks).max(-1, keepdims=True)
    byte = np.maximum(np.where(amax > 0, np.frexp(amax)[1] - 1 + 127, 0) - down, 1)
    scale = np.exp2(byte - 127.0)
    codes = (blocks / scale).astype(np.float32).astype(dtype).astype(np.float64)
    return np.moveaxis((codes * scale).reshape(v.shape), -1, axis)


WIDE = False


def mx_kscale(k):
    if not WIDE:
        return np.ones(k)
    levels = np.array([10, -10, 5, -5, 0])
    a = np.random.permutation(np.resize(levels, k // 512 * 4)).reshape(k // 512, 4)
    idx = np.arange(k)
    return np.exp2(a[idx // 512, idx % 128 // 32])


BF16 = ml_dtypes.bfloat16


def bf(x):
    return np.asarray(x, np.float32).astype(BF16)


def f64(x):
    return np.asarray(x).astype(np.float64)


N, D, K, R, ITERS = 16384, 512, 128, 3, 2
BETA = 5.0
NOISE = 0.7
KAPPA = 2.5


def softmax_rows(v):
    e = np.exp(v - v.max(axis=1, keepdims=True))
    return e / e.sum(axis=1, keepdims=True)


def unit_rows(v):
    return v / np.sqrt((v * v).sum(axis=1, keepdims=True))


def setup_inputs():
    t = mx_kscale(D)[::D // K]
    z = np.random.standard_normal((N, R))
    x = z @ np.random.standard_normal((R, D)) + NOISE * np.random.standard_normal((N, D))
    m = np.random.standard_normal((K, R))
    r = softmax_rows(KAPPA * (unit_rows(z) @ unit_rows(m).T) + 0.5 * np.random.standard_normal((N, K)))
    return {"x1": bf(x / np.sqrt(D * (R + NOISE * NOISE))), "r": bf(r * t[None, :])}


def reference(x1, r):
    x1, r = f64(x1), f64(r)
    xn = x1 / np.sqrt((x1 * x1).sum(axis=1, keepdims=True))
    cluster_r = r.sum(axis=0)
    mu = (mxq(r, 0, "e4m3").T @ mxq(xn, 0, "e4m3")) / cluster_r[:, None]
    r_new = softmax_rows(BETA * (mxq(xn, 1, "e4m3") @ mxq(mu, 1, "e4m3").T))
    return mu, r_new

@@ -1,0 +1,218 @@
+from contextlib import ExitStack
+
+import concourse.mybir as mybir
+from concourse.masks import make_identity
+
+F32 = mybir.dt.float32
+BF16 = mybir.dt.bfloat16
+U32 = mybir.dt.uint32
+U8 = mybir.dt.uint8
+FP8X4 = mybir.dt.float8_e4m3fn_x4
+ACT = mybir.ActivationFunctionType
+ALU = mybir.AluOpType
+AXIS = mybir.AxisListType
+
+P = 128
+PACK = 4
+K_PASS = P * PACK
+
+ROWS = 16384
+FEATURES = 512
+CENTROIDS = 128
+BETA = 5.0
+
+PASSES = ROWS // K_PASS
+R_CHUNK = 4
+HALVES = 2
+ONES_COLS = 32
+
+FLOPS = 2 * 2 * ROWS * FEATURES * CENTROIDS
+
+
+def tile_clusternet_pb_k_kernel(tc, x1, r, out_0, out_1):
+    nc = tc.nc
+
+    x_rows = x1.rearrange("(g p j) f -> g p j f", p=P, j=PACK)
+    r_rows = r.rearrange("(q g p j) c -> q p g (j c)", g=R_CHUNK, p=P, j=PACK)
+    out_rows = out_1.rearrange("(g p j) c -> g p (j c)", p=P, j=PACK)
+
+    with ExitStack() as ctx:
+        const = ctx.enter_context(tc.tile_pool(name="const", bufs=1))
+        keep = ctx.enter_context(tc.tile_pool(name="keep", bufs=1))
+        x_pool = ctx.enter_context(tc.tile_pool(name="x", bufs=6))
+        r_pool = ctx.enter_context(tc.tile_pool(name="r", bufs=2))
+        scrap = ctx.enter_context(tc.tile_pool(name="scrap", bufs=4))
+        stage = ctx.enter_context(tc.tile_pool(name="stage", bufs=3))
+        stats = ctx.enter_context(tc.tile_pool(name="stats", bufs=6))
+        probs = ctx.enter_context(tc.tile_pool(name="probs", bufs=4))
+        sums = ctx.enter_context(tc.psum_pool(name="sums", bufs=1))
+
+        ident = const.tile([P, P], F32)
+        make_identity(nc, ident[:])
+        ones = const.tile([P, ONES_COLS], BF16)
+        nc.vector.memset(ones[:], 1.0)
+
+        xt_codes = keep.tile([P, PASSES, K_PASS], U32, align_bytes=64)
+        xt_scales = keep.tile([P, PASSES, K_PASS], U8, align_bytes=64)
+
+        mu_sum = sums.tile([CENTROIDS, FEATURES], F32)
+        r_sum = sums.tile([CENTROIDS, ONES_COLS], F32)
+
+        with tc.psum_pool(name="turned", bufs=6) as turned:
+            for g in range(PASSES):
+                x_t = x_pool.tile([P, PACK, FEATURES], BF16)
+                nc.sync.dma_start(out=x_t[:], in_=x_rows[g])
+
+                gg = g % R_CHUNK
+                if gg == 0:
+                    r_t = r_pool.tile([P, R_CHUNK, PACK, CENTROIDS], BF16)
+                    nc.sync.dma_start(
+                        out=r_t[:].rearrange("p g j c -> p g (j c)"), in_=r_rows[g // R_CHUNK]
+                    )
+                    r_grouped = r_pool.tile([P, R_CHUNK, CENTROIDS, PACK], BF16, align_bytes=64)
+                    nc.vector.tensor_copy(
+                        out=r_grouped[:].rearrange("p g (c i) j -> p g c j i", i=4),
+                        in_=r_t[:].rearrange("p g j (c i) -> p g c j i", i=4),
+                    )
+                    r_codes = r_pool.tile([P, R_CHUNK, CENTROIDS], U32, align_bytes=64)
+                    r_scales = r_pool.tile([P, R_CHUNK, CENTROIDS], U8, align_bytes=64)
+                    nc.vector.quantize_mx(
+                        out=r_codes[:].rearrange("p g c -> p (g c)").bitcast(FP8X4),
+                        scales=r_scales[:].rearrange("p g c -> p (g c)"),
+                        in_=r_grouped[:].rearrange("p g c j -> p (g c j)"),
+                    )
+
+                for j in range(PACK):
+                    nc.tensor.matmul(
+                        out=r_sum[:],
+                        lhsT=r_t[:, gg, j, :],
+                        rhs=ones[:],
+                        start=(g == 0 and j == 0),
+                        stop=(g == PASSES - 1 and j == PACK - 1),
+                    )
+
+                sum_sq = stats.tile([P, PACK], F32)
+                for j in range(PACK):
+                    squares = scrap.tile([P, FEATURES], BF16)
+                    nc.scalar.activation(
+                        out=squares[:],
+                        in_=x_t[:, j, :],
+                        func=ACT.Square,
+                        accum_out=sum_sq[:, j : j + 1],
+                    )
+                norm = stats.tile([P, PACK], F32)
+                nc.scalar.sqrt(out=norm[:], in_=sum_sq[:])
+                inv_norm = stats.tile([P, PACK], F32)
+                nc.vector.reciprocal(out=inv_norm[:], in_=norm[:])
+
+                for j in range(PACK):
+                    nc.vector.tensor_scalar_mul(
+                        out=x_t[:, j, :], in0=x_t[:, j, :], scalar1=inv_norm[:, j : j + 1]
+                    )
+
+                x_grouped = stage.tile([P, FEATURES, PACK], BF16, align_bytes=64)
+                nc.vector.tensor_copy(
+                    out=x_grouped[:].rearrange("p (f i) j -> p f j i", i=4),
+                    in_=x_t[:].rearrange("p j (f i) -> p f j i", i=4),
+                )
+                x_codes = stage.tile([P, FEATURES], U32, align_bytes=64)
+                x_scales = stage.tile([P, FEATURES], U8, align_bytes=64)
+                nc.vector.quantize_mx(
+                    out=x_codes[:].bitcast(FP8X4),
+                    scales=x_scales[:],
+                    in_=x_grouped[:].rearrange("p f j -> p (f j)"),
+                )
+                nc.tensor.matmul_mx(
+                    out=mu_sum[:],
+                    lhsT=r_codes[:, gg, :].bitcast(FP8X4),
+                    lhsT_scale=r_scales[:, gg, :],
+                    rhs=x_codes[:].bitcast(FP8X4),
+                    rhs_scale=x_scales[:],
+                    start=(g == 0),
+                    stop=(g == PASSES - 1),
+                )
+
+                x_words = x_t[:].bitcast(F32)
+                xt_grouped = stage.tile([P, PACK, P, PACK], BF16, align_bytes=64)
+                xt_words = xt_grouped[:].bitcast(F32)
+                for b in range(PACK // 2):
+                    bank = turned.tile([P, 2, HALVES, P], F32)
+                    for jj in range(2):
+                        for u in range(HALVES):
+                            nc.tensor.transpose(
+                                bank[:, jj, u, :],
+                                x_words[:, 2 * b + jj, u * P : (u + 1) * P],
+                                ident[:],
+                            )
+                    nc.scalar.copy(
+                        out=xt_words[:, 2 * b : 2 * b + 2, :, :],
+                        in_=bank[:].rearrange("p j u m -> p j m u"),
+                    )
+                nc.vector.quantize_mx(
+                    out=xt_codes[:, g, :].bitcast(FP8X4),
+                    scales=xt_scales[:, g, :],
+                    in_=xt_grouped[:].rearrange("p j m t -> p (j m t)"),
+                )
+
+        with tc.psum_pool(name="scores", bufs=5) as scores, tc.psum_pool(
+            name="mu_turned", bufs=1
+        ) as mu_turned:
+            inv_r_sum = const.tile([CENTROIDS, 1], F32)
+            nc.vector.reciprocal(out=inv_r_sum[:], in_=r_sum[:, 0:1])
+            mu = const.tile([CENTROIDS, FEATURES], F32)
+            nc.vector.tensor_scalar_mul(out=mu[:], in0=mu_sum[:], scalar1=inv_r_sum[:])
+            nc.sync.dma_start(out=out_0, in_=mu[:])
+            mu_bf = const.tile([CENTROIDS, FEATURES], BF16)
+            nc.vector.tensor_copy(out=mu_bf[:], in_=mu[:])
+
+            mu_words = mu_bf[:].bitcast(F32)
+            mu_bank = mu_turned.tile([P, HALVES, CENTROIDS], F32)
+            for u in range(HALVES):
+                nc.tensor.transpose(mu_bank[:, u, :], mu_words[:, u * P : (u + 1) * P], ident[:])
+            mu_grouped = const.tile([P, CENTROIDS, PACK], BF16, align_bytes=64)
+            nc.vector.tensor_copy(
+                out=mu_grouped[:].bitcast(F32), in_=mu_bank[:].rearrange("p u c -> p c u")
+            )
+            mu_codes = const.tile([P, CENTROIDS], U32, align_bytes=64)
+            mu_scales = const.tile([P, CENTROIDS], U8, align_bytes=64)
+            nc.vector.quantize_mx(
+                out=mu_codes[:].bitcast(FP8X4),
+                scales=mu_scales[:],
+                in_=mu_grouped[:].rearrange("p c t -> p (c t)"),
+            )
+
+            for g in range(PASSES):
+                score = scores.tile([P, PACK, CENTROIDS], F32)
+                for j in range(PACK):
+                    cols = slice(j * P, (j + 1) * P)
+                    nc.tensor.matmul_mx(
+                        out=score[:, j, :],
+                        lhsT=xt_codes[:, g, cols].bitcast(FP8X4),
+                        lhsT_scale=xt_scales[:, g, cols],
+                        rhs=mu_codes[:].bitcast(FP8X4),
+                        rhs_scale=mu_scales[:],
+                        start=True,
+                        stop=True,
+                    )
+                top = stats.tile([P, PACK], F32)
+                nc.vector.tensor_reduce(out=top[:], in_=score[:], axis=AXIS.X, op=ALU.max)
+                shift = stats.tile([P, PACK], F32)
+                nc.vector.tensor_scalar_mul(out=shift[:], in0=top[:], scalar1=-BETA)
+                prob = probs.tile([P, PACK, CENTROIDS], F32)
+                total = stats.tile([P, PACK], F32)
+                for j in range(PACK):
+                    nc.scalar.activation(
+                        out=prob[:, j, :],
+                        in_=score[:, j, :],
+                        func=ACT.Exp,
+                        bias=shift[:, j : j + 1],
+                        scale=BETA,
+                        accum_out=total[:, j : j + 1],
+                    )
+                inv_total = stats.tile([P, PACK], F32)
+                nc.vector.reciprocal(out=inv_total[:], in_=total[:])
+                for j in range(PACK):
+                    nc.vector.tensor_scalar_mul(
+                        out=prob[:, j, :], in0=prob[:, j, :], scalar1=inv_total[:, j : j + 1]
+                    )
+                nc.sync.dma_start(out=out_rows[g], in_=prob[:].rearrange("p j c -> p (j c)"))

@@ -26,6 +26,9 @@ R_CHUNK = 4
 HALVES = 2
 ONES_COLS = 32
 
+LOAD_AHEAD = 3
+TURN_LAG = 2
+
 FLOPS = 2 * 2 * ROWS * FEATURES * CENTROIDS
 
 
@@ -39,124 +42,152 @@ def tile_clusternet_pb_k_kernel(tc, x1, r, out_0, out_1):
     with ExitStack() as ctx:
         const = ctx.enter_context(tc.tile_pool(name="const", bufs=1))
         keep = ctx.enter_context(tc.tile_pool(name="keep", bufs=1))
-        x_pool = ctx.enter_context(tc.tile_pool(name="x", bufs=6))
-        r_pool = ctx.enter_context(tc.tile_pool(name="r", bufs=2))
+        x_pool = ctx.enter_context(tc.tile_pool(name="x", bufs=LOAD_AHEAD + TURN_LAG + 2))
+        r_pool = ctx.enter_context(tc.tile_pool(name="r", bufs=3))
+        r_stage = ctx.enter_context(tc.tile_pool(name="r_stage", bufs=2))
         scrap = ctx.enter_context(tc.tile_pool(name="scrap", bufs=4))
         stage = ctx.enter_context(tc.tile_pool(name="stage", bufs=3))
-        stats = ctx.enter_context(tc.tile_pool(name="stats", bufs=6))
+        stats = ctx.enter_context(tc.tile_pool(name="stats", bufs=4))
         probs = ctx.enter_context(tc.tile_pool(name="probs", bufs=4))
         sums = ctx.enter_context(tc.psum_pool(name="sums", bufs=1))
+        turned = ctx.enter_context(tc.psum_pool(name="turned", bufs=4))
+        scores = ctx.enter_context(tc.psum_pool(name="scores", bufs=2))
+        ctx.enter_context(tc.manual_schedule())
 
         ident = const.tile([P, P], F32)
         make_identity(nc, ident[:])
         ones = const.tile([P, ONES_COLS], BF16)
         nc.vector.memset(ones[:], 1.0)
+        warm = const.tile([P, 1], F32)
+        nc.vector.memset(warm[:], 1.0)
+        nc.scalar.sqrt(out=warm[:], in_=warm[:])
 
         xt_codes = keep.tile([P, PASSES, K_PASS], U32, align_bytes=64)
         xt_scales = keep.tile([P, PASSES, K_PASS], U8, align_bytes=64)
+        mu_codes = keep.tile([P, CENTROIDS], U32, align_bytes=64)
+        mu_scales = keep.tile([P, CENTROIDS], U8, align_bytes=64)
 
         mu_sum = sums.tile([CENTROIDS, FEATURES], F32)
         r_sum = sums.tile([CENTROIDS, ONES_COLS], F32)
 
-        with tc.psum_pool(name="turned", bufs=6) as turned:
-            for g in range(PASSES):
-                x_t = x_pool.tile([P, PACK, FEATURES], BF16)
-                nc.sync.dma_start(out=x_t[:], in_=x_rows[g])
+        x_of, norm_of, x_grouped_of, x_codes_of, banks_of, xt_grouped_of = {}, {}, {}, {}, {}, {}
+        r_of, r_codes_of = {}, {}
+        score_of, shift_of, prob_of, total_of = {}, {}, {}, {}
 
-                gg = g % R_CHUNK
-                if gg == 0:
-                    r_t = r_pool.tile([P, R_CHUNK, PACK, CENTROIDS], BF16)
-                    nc.sync.dma_start(
-                        out=r_t[:].rearrange("p g j c -> p g (j c)"), in_=r_rows[g // R_CHUNK]
-                    )
-                    r_grouped = r_pool.tile([P, R_CHUNK, CENTROIDS, PACK], BF16, align_bytes=64)
-                    nc.vector.tensor_copy(
-                        out=r_grouped[:].rearrange("p g (c i) j -> p g c j i", i=4),
-                        in_=r_t[:].rearrange("p g j (c i) -> p g c j i", i=4),
-                    )
-                    r_codes = r_pool.tile([P, R_CHUNK, CENTROIDS], U32, align_bytes=64)
-                    r_scales = r_pool.tile([P, R_CHUNK, CENTROIDS], U8, align_bytes=64)
-                    nc.vector.quantize_mx(
-                        out=r_codes[:].rearrange("p g c -> p (g c)").bitcast(FP8X4),
-                        scales=r_scales[:].rearrange("p g c -> p (g c)"),
-                        in_=r_grouped[:].rearrange("p g c j -> p (g c j)"),
-                    )
+        def load(g):
+            x_of[g] = x_pool.tile([P, PACK, FEATURES], BF16, name="x_t")
+            nc.sync.dma_start(out=x_of[g][:], in_=x_rows[g])
+            if g % R_CHUNK == 0:
+                q = g // R_CHUNK
+                r_of[q] = r_pool.tile([P, R_CHUNK, PACK, CENTROIDS], BF16, name="r_t")
+                nc.sync.dma_start(out=r_of[q][:].rearrange("p g j c -> p g (j c)"), in_=r_rows[q])
 
-                for j in range(PACK):
-                    nc.tensor.matmul(
-                        out=r_sum[:],
-                        lhsT=r_t[:, gg, j, :],
-                        rhs=ones[:],
-                        start=(g == 0 and j == 0),
-                        stop=(g == PASSES - 1 and j == PACK - 1),
-                    )
+        def quantise_r(q):
+            r_grouped = r_stage.tile([P, R_CHUNK, CENTROIDS, PACK], BF16, align_bytes=64)
+            nc.vector.tensor_copy(
+                out=r_grouped[:].rearrange("p g (c i) j -> p g c j i", i=4),
+                in_=r_of[q][:].rearrange("p g j (c i) -> p g c j i", i=4),
+            )
+            r_codes = r_stage.tile([P, R_CHUNK, CENTROIDS], U32, align_bytes=64)
+            r_scales = r_stage.tile([P, R_CHUNK, CENTROIDS], U8, align_bytes=64)
+            nc.vector.quantize_mx(
+                out=r_codes[:].rearrange("p g c -> p (g c)").bitcast(FP8X4),
+                scales=r_scales[:].rearrange("p g c -> p (g c)"),
+                in_=r_grouped[:].rearrange("p g c j -> p (g c j)"),
+            )
+            r_codes_of[q] = (r_codes, r_scales)
 
-                sum_sq = stats.tile([P, PACK], F32)
-                for j in range(PACK):
-                    squares = scrap.tile([P, FEATURES], BF16)
-                    nc.scalar.activation(
-                        out=squares[:],
-                        in_=x_t[:, j, :],
-                        func=ACT.Square,
-                        accum_out=sum_sq[:, j : j + 1],
-                    )
-                norm = stats.tile([P, PACK], F32)
-                nc.scalar.sqrt(out=norm[:], in_=sum_sq[:])
-                inv_norm = stats.tile([P, PACK], F32)
-                nc.vector.reciprocal(out=inv_norm[:], in_=norm[:])
-
-                for j in range(PACK):
-                    nc.vector.tensor_scalar_mul(
-                        out=x_t[:, j, :], in0=x_t[:, j, :], scalar1=inv_norm[:, j : j + 1]
-                    )
-
-                x_grouped = stage.tile([P, FEATURES, PACK], BF16, align_bytes=64)
-                nc.vector.tensor_copy(
-                    out=x_grouped[:].rearrange("p (f i) j -> p f j i", i=4),
-                    in_=x_t[:].rearrange("p j (f i) -> p f j i", i=4),
+        def norms(g):
+            sum_sq = stats.tile([P, PACK], F32)
+            for j in range(PACK):
+                squares = scrap.tile([P, FEATURES], BF16)
+                nc.scalar.activation(
+                    out=squares[:],
+                    in_=x_of[g][:, j, :],
+                    func=ACT.Square,
+                    accum_out=sum_sq[:, j : j + 1],
                 )
-                x_codes = stage.tile([P, FEATURES], U32, align_bytes=64)
-                x_scales = stage.tile([P, FEATURES], U8, align_bytes=64)
-                nc.vector.quantize_mx(
-                    out=x_codes[:].bitcast(FP8X4),
-                    scales=x_scales[:],
-                    in_=x_grouped[:].rearrange("p f j -> p (f j)"),
-                )
-                nc.tensor.matmul_mx(
-                    out=mu_sum[:],
-                    lhsT=r_codes[:, gg, :].bitcast(FP8X4),
-                    lhsT_scale=r_scales[:, gg, :],
-                    rhs=x_codes[:].bitcast(FP8X4),
-                    rhs_scale=x_scales[:],
-                    start=(g == 0),
-                    stop=(g == PASSES - 1),
+            norm = stats.tile([P, PACK], F32)
+            nc.scalar.sqrt(out=norm[:], in_=sum_sq[:])
+            norm_of[g] = norm
+
+        def scale(g):
+            inv_norm = stats.tile([P, PACK], F32)
+            nc.vector.reciprocal(out=inv_norm[:], in_=norm_of[g][:])
+            for j in range(PACK):
+                nc.vector.tensor_scalar_mul(
+                    out=x_of[g][:, j, :], in0=x_of[g][:, j, :], scalar1=inv_norm[:, j : j + 1]
                 )
 
-                x_words = x_t[:].bitcast(F32)
-                xt_grouped = stage.tile([P, PACK, P, PACK], BF16, align_bytes=64)
-                xt_words = xt_grouped[:].bitcast(F32)
-                for b in range(PACK // 2):
-                    bank = turned.tile([P, 2, HALVES, P], F32)
-                    for jj in range(2):
-                        for u in range(HALVES):
-                            nc.tensor.transpose(
-                                bank[:, jj, u, :],
-                                x_words[:, 2 * b + jj, u * P : (u + 1) * P],
-                                ident[:],
-                            )
-                    nc.scalar.copy(
-                        out=xt_words[:, 2 * b : 2 * b + 2, :, :],
-                        in_=bank[:].rearrange("p j u m -> p j m u"),
-                    )
-                nc.vector.quantize_mx(
-                    out=xt_codes[:, g, :].bitcast(FP8X4),
-                    scales=xt_scales[:, g, :],
-                    in_=xt_grouped[:].rearrange("p j m t -> p (j m t)"),
+        def regroup(g):
+            x_grouped_of[g] = stage.tile([P, FEATURES, PACK], BF16, align_bytes=64, name="x_grouped")
+            nc.vector.tensor_copy(
+                out=x_grouped_of[g][:].rearrange("p (f i) j -> p f j i", i=4),
+                in_=x_of[g][:].rearrange("p j (f i) -> p f j i", i=4),
+            )
+
+        def quantise_rows(g):
+            x_codes = stage.tile([P, FEATURES], U32, align_bytes=64)
+            x_scales = stage.tile([P, FEATURES], U8, align_bytes=64)
+            nc.vector.quantize_mx(
+                out=x_codes[:].bitcast(FP8X4),
+                scales=x_scales[:],
+                in_=x_grouped_of[g][:].rearrange("p f j -> p (f j)"),
+            )
+            x_codes_of[g] = (x_codes, x_scales)
+
+        def row_pass(g):
+            q, gg = divmod(g, R_CHUNK)
+            r_codes, r_scales = r_codes_of[q]
+            x_codes, x_scales = x_codes_of[g]
+            for j in range(PACK):
+                nc.tensor.matmul(
+                    out=r_sum[:],
+                    lhsT=r_of[q][:, gg, j, :],
+                    rhs=ones[:],
+                    start=(g == 0 and j == 0),
+                    stop=(g == PASSES - 1 and j == PACK - 1),
+                )
+            nc.tensor.matmul_mx(
+                out=mu_sum[:],
+                lhsT=r_codes[:, gg, :].bitcast(FP8X4),
+                lhsT_scale=r_scales[:, gg, :],
+                rhs=x_codes[:].bitcast(FP8X4),
+                rhs_scale=x_scales[:],
+                start=(g == 0),
+                stop=(g == PASSES - 1),
+            )
+
+        def turn(g):
+            x_words = x_of[g][:].bitcast(F32)
+            banks_of[g] = []
+            for b in range(PACK // 2):
+                bank = turned.tile([P, 2, HALVES, P], F32)
+                for jj in range(2):
+                    for u in range(HALVES):
+                        nc.tensor.transpose(
+                            bank[:, jj, u, :], x_words[:, 2 * b + jj, u * P : (u + 1) * P], ident[:]
+                        )
+                banks_of[g].append(bank)
+
+        def empty(g):
+            xt_grouped_of[g] = stage.tile([P, PACK, P, PACK], BF16, align_bytes=64, name="xt_grouped")
+            xt_words = xt_grouped_of[g][:].bitcast(F32)
+            for b in range(PACK // 2):
+                nc.scalar.copy(
+                    out=xt_words[:, 2 * b : 2 * b + 2, :, :],
+                    in_=banks_of[g][b][:].rearrange("p j u m -> p j m u"),
                 )
 
-        with tc.psum_pool(name="scores", bufs=5) as scores, tc.psum_pool(
-            name="mu_turned", bufs=1
-        ) as mu_turned:
+        def quantise_features(g):
+            nc.vector.quantize_mx(
+                out=xt_codes[:, g, :].bitcast(FP8X4),
+                scales=xt_scales[:, g, :],
+                in_=xt_grouped_of[g][:].rearrange("p j m t -> p (j m t)"),
+            )
+
+        def centroids():
+            nc.scalar.activation(out=warm[:], in_=warm[:], func=ACT.Exp)
             inv_r_sum = const.tile([CENTROIDS, 1], F32)
             nc.vector.reciprocal(out=inv_r_sum[:], in_=r_sum[:, 0:1])
             mu = const.tile([CENTROIDS, FEATURES], F32)
@@ -164,55 +195,85 @@ def tile_clusternet_pb_k_kernel(tc, x1, r, out_0, out_1):
             nc.sync.dma_start(out=out_0, in_=mu[:])
             mu_bf = const.tile([CENTROIDS, FEATURES], BF16)
             nc.vector.tensor_copy(out=mu_bf[:], in_=mu[:])
-
             mu_words = mu_bf[:].bitcast(F32)
-            mu_bank = mu_turned.tile([P, HALVES, CENTROIDS], F32)
+            mu_bank = turned.tile([P, HALVES, CENTROIDS], F32, tag="bank")
             for u in range(HALVES):
                 nc.tensor.transpose(mu_bank[:, u, :], mu_words[:, u * P : (u + 1) * P], ident[:])
             mu_grouped = const.tile([P, CENTROIDS, PACK], BF16, align_bytes=64)
             nc.vector.tensor_copy(
                 out=mu_grouped[:].bitcast(F32), in_=mu_bank[:].rearrange("p u c -> p c u")
             )
-            mu_codes = const.tile([P, CENTROIDS], U32, align_bytes=64)
-            mu_scales = const.tile([P, CENTROIDS], U8, align_bytes=64)
             nc.vector.quantize_mx(
                 out=mu_codes[:].bitcast(FP8X4),
                 scales=mu_scales[:],
                 in_=mu_grouped[:].rearrange("p c t -> p (c t)"),
             )
 
-            for g in range(PASSES):
-                score = scores.tile([P, PACK, CENTROIDS], F32)
-                for j in range(PACK):
-                    cols = slice(j * P, (j + 1) * P)
-                    nc.tensor.matmul_mx(
-                        out=score[:, j, :],
-                        lhsT=xt_codes[:, g, cols].bitcast(FP8X4),
-                        lhsT_scale=xt_scales[:, g, cols],
-                        rhs=mu_codes[:].bitcast(FP8X4),
-                        rhs_scale=mu_scales[:],
-                        start=True,
-                        stop=True,
-                    )
-                top = stats.tile([P, PACK], F32)
-                nc.vector.tensor_reduce(out=top[:], in_=score[:], axis=AXIS.X, op=ALU.max)
-                shift = stats.tile([P, PACK], F32)
-                nc.vector.tensor_scalar_mul(out=shift[:], in0=top[:], scalar1=-BETA)
-                prob = probs.tile([P, PACK, CENTROIDS], F32)
-                total = stats.tile([P, PACK], F32)
-                for j in range(PACK):
-                    nc.scalar.activation(
-                        out=prob[:, j, :],
-                        in_=score[:, j, :],
-                        func=ACT.Exp,
-                        bias=shift[:, j : j + 1],
-                        scale=BETA,
-                        accum_out=total[:, j : j + 1],
-                    )
-                inv_total = stats.tile([P, PACK], F32)
-                nc.vector.reciprocal(out=inv_total[:], in_=total[:])
-                for j in range(PACK):
-                    nc.vector.tensor_scalar_mul(
-                        out=prob[:, j, :], in0=prob[:, j, :], scalar1=inv_total[:, j : j + 1]
-                    )
-                nc.sync.dma_start(out=out_rows[g], in_=prob[:].rearrange("p j c -> p (j c)"))
+        def score(g):
+            score_of[g] = scores.tile([P, PACK, CENTROIDS], F32, name="score")
+            for j in range(PACK):
+                cols = slice(j * P, (j + 1) * P)
+                nc.tensor.matmul_mx(
+                    out=score_of[g][:, j, :],
+                    lhsT=xt_codes[:, g, cols].bitcast(FP8X4),
+                    lhsT_scale=xt_scales[:, g, cols],
+                    rhs=mu_codes[:].bitcast(FP8X4),
+                    rhs_scale=mu_scales[:],
+                    start=True,
+                    stop=True,
+                )
+
+        def find_shift(g):
+            top = stats.tile([P, PACK], F32)
+            nc.vector.tensor_reduce(out=top[:], in_=score_of[g][:], axis=AXIS.X, op=ALU.max)
+            shift_of[g] = stats.tile([P, PACK], F32, name="shift")
+            nc.vector.tensor_scalar_mul(out=shift_of[g][:], in0=top[:], scalar1=-BETA)
+
+        def exponentials(g):
+            prob_of[g] = probs.tile([P, PACK, CENTROIDS], F32, name="prob")
+            total_of[g] = stats.tile([P, PACK], F32, name="total")
+            for j in range(PACK):
+                nc.scalar.activation(
+                    out=prob_of[g][:, j, :],
+                    in_=score_of[g][:, j, :],
+                    func=ACT.Exp,
+                    bias=shift_of[g][:, j : j + 1],
+                    scale=BETA,
+                    accum_out=total_of[g][:, j : j + 1],
+                )
+
+        def normalise(g):
+            inv_total = stats.tile([P, PACK], F32)
+            nc.vector.reciprocal(out=inv_total[:], in_=total_of[g][:])
+            for j in range(PACK):
+                nc.vector.tensor_scalar_mul(
+                    out=prob_of[g][:, j, :], in0=prob_of[g][:, j, :], scalar1=inv_total[:, j : j + 1]
+                )
+            nc.sync.dma_start(out=out_rows[g], in_=prob_of[g][:].rearrange("p j c -> p (j c)"))
+
+        def do(step, g):
+            if 0 <= g < PASSES:
+                step(g)
+
+        for g in range(LOAD_AHEAD):
+            load(g)
+        quantise_r(0)
+        first_score = PASSES + 1
+        for i in range(first_score + PASSES + 1):
+            do(load, i + LOAD_AHEAD)
+            do(norms, i)
+            do(scale, i - 1)
+            do(turn, i - TURN_LAG)
+            do(empty, i - TURN_LAG)
+            do(regroup, i - 1)
+            do(quantise_features, i - TURN_LAG - 1)
+            do(quantise_rows, i - 1)
+            do(row_pass, i - 1)
+            if (i + 1) % R_CHUNK == 0 and i + 1 < PASSES:
+                quantise_r((i + 1) // R_CHUNK)
+            if i == PASSES:
+                centroids()
+            do(score, i - first_score)
+            do(find_shift, i - first_score)
+            do(exponentials, i - first_score)
+            do(normalise, i - first_score - 1)

@@ -26,8 +26,8 @@ R_CHUNK = 4
 HALVES = 2
 ONES_COLS = 32
 
-LOAD_AHEAD = 3
-TURN_LAG = 2
+LOAD_AHEAD = 4
+TURN_LAG = 4
 
 FLOPS = 2 * 2 * ROWS * FEATURES * CENTROIDS
 
@@ -48,10 +48,10 @@ def tile_clusternet_pb_k_kernel(tc, x1, r, out_0, out_1):
         scrap = ctx.enter_context(tc.tile_pool(name="scrap", bufs=4))
         stage = ctx.enter_context(tc.tile_pool(name="stage", bufs=3))
         stats = ctx.enter_context(tc.tile_pool(name="stats", bufs=4))
-        probs = ctx.enter_context(tc.tile_pool(name="probs", bufs=4))
+        probs = ctx.enter_context(tc.tile_pool(name="probs", bufs=6))
         sums = ctx.enter_context(tc.psum_pool(name="sums", bufs=1))
-        turned = ctx.enter_context(tc.psum_pool(name="turned", bufs=4))
-        scores = ctx.enter_context(tc.psum_pool(name="scores", bufs=2))
+        turned = ctx.enter_context(tc.psum_pool(name="turned", bufs=3))
+        scores = ctx.enter_context(tc.psum_pool(name="scores", bufs=3))
         ctx.enter_context(tc.manual_schedule())
 
         ident = const.tile([P, P], F32)
@@ -70,9 +70,10 @@ def tile_clusternet_pb_k_kernel(tc, x1, r, out_0, out_1):
         mu_sum = sums.tile([CENTROIDS, FEATURES], F32)
         r_sum = sums.tile([CENTROIDS, ONES_COLS], F32)
 
-        x_of, norm_of, x_grouped_of, x_codes_of, banks_of, xt_grouped_of = {}, {}, {}, {}, {}, {}
-        r_of, r_codes_of = {}, {}
-        score_of, shift_of, prob_of, total_of = {}, {}, {}, {}
+        x_of, sum_sq_of, norm_of, inv_norm_of = {}, {}, {}, {}
+        x_grouped_of, x_codes_of, banks_of, xt_grouped_of = {}, {}, {}, {}
+        r_of, r_grouped_of, r_codes_of = {}, {}, {}
+        score_of, top_of, shift_of, prob_of, total_of, inv_total_of = {}, {}, {}, {}, {}, {}
 
         def load(g):
             x_of[g] = x_pool.tile([P, PACK, FEATURES], BF16, name="x_t")
@@ -82,41 +83,48 @@ def tile_clusternet_pb_k_kernel(tc, x1, r, out_0, out_1):
                 r_of[q] = r_pool.tile([P, R_CHUNK, PACK, CENTROIDS], BF16, name="r_t")
                 nc.sync.dma_start(out=r_of[q][:].rearrange("p g j c -> p g (j c)"), in_=r_rows[q])
 
-        def quantise_r(q):
-            r_grouped = r_stage.tile([P, R_CHUNK, CENTROIDS, PACK], BF16, align_bytes=64)
+        def regroup_r(q):
+            r_grouped_of[q] = r_stage.tile(
+                [P, R_CHUNK, CENTROIDS, PACK], BF16, align_bytes=64, name="r_grouped"
+            )
             nc.vector.tensor_copy(
-                out=r_grouped[:].rearrange("p g (c i) j -> p g c j i", i=4),
+                out=r_grouped_of[q][:].rearrange("p g (c i) j -> p g c j i", i=4),
                 in_=r_of[q][:].rearrange("p g j (c i) -> p g c j i", i=4),
             )
+
+        def quantise_r(q):
             r_codes = r_stage.tile([P, R_CHUNK, CENTROIDS], U32, align_bytes=64)
             r_scales = r_stage.tile([P, R_CHUNK, CENTROIDS], U8, align_bytes=64)
             nc.vector.quantize_mx(
                 out=r_codes[:].rearrange("p g c -> p (g c)").bitcast(FP8X4),
                 scales=r_scales[:].rearrange("p g c -> p (g c)"),
-                in_=r_grouped[:].rearrange("p g c j -> p (g c j)"),
+                in_=r_grouped_of[q][:].rearrange("p g c j -> p (g c j)"),
             )
             r_codes_of[q] = (r_codes, r_scales)
 
-        def norms(g):
-            sum_sq = stats.tile([P, PACK], F32)
+        def squares_of(g):
+            sum_sq_of[g] = stats.tile([P, PACK], F32, name="sum_sq")
             for j in range(PACK):
                 squares = scrap.tile([P, FEATURES], BF16)
                 nc.scalar.activation(
                     out=squares[:],
                     in_=x_of[g][:, j, :],
                     func=ACT.Square,
-                    accum_out=sum_sq[:, j : j + 1],
+                    accum_out=sum_sq_of[g][:, j : j + 1],
                 )
-            norm = stats.tile([P, PACK], F32)
-            nc.scalar.sqrt(out=norm[:], in_=sum_sq[:])
-            norm_of[g] = norm
+
+        def root(g):
+            norm_of[g] = stats.tile([P, PACK], F32, name="norm")
+            nc.scalar.sqrt(out=norm_of[g][:], in_=sum_sq_of[g][:])
+
+        def invert(g):
+            inv_norm_of[g] = stats.tile([P, PACK], F32, name="inv_norm")
+            nc.vector.reciprocal(out=inv_norm_of[g][:], in_=norm_of[g][:])
 
         def scale(g):
-            inv_norm = stats.tile([P, PACK], F32)
-            nc.vector.reciprocal(out=inv_norm[:], in_=norm_of[g][:])
             for j in range(PACK):
                 nc.vector.tensor_scalar_mul(
-                    out=x_of[g][:, j, :], in0=x_of[g][:, j, :], scalar1=inv_norm[:, j : j + 1]
+                    out=x_of[g][:, j, :], in0=x_of[g][:, j, :], scalar1=inv_norm_of[g][:, j : j + 1]
                 )
 
         def regroup(g):
@@ -136,10 +144,8 @@ def tile_clusternet_pb_k_kernel(tc, x1, r, out_0, out_1):
             )
             x_codes_of[g] = (x_codes, x_scales)
 
-        def row_pass(g):
+        def sum_r(g):
             q, gg = divmod(g, R_CHUNK)
-            r_codes, r_scales = r_codes_of[q]
-            x_codes, x_scales = x_codes_of[g]
             for j in range(PACK):
                 nc.tensor.matmul(
                     out=r_sum[:],
@@ -148,6 +154,11 @@ def tile_clusternet_pb_k_kernel(tc, x1, r, out_0, out_1):
                     start=(g == 0 and j == 0),
                     stop=(g == PASSES - 1 and j == PACK - 1),
                 )
+
+        def row_pass(g):
+            q, gg = divmod(g, R_CHUNK)
+            r_codes, r_scales = r_codes_of[q]
+            x_codes, x_scales = x_codes_of[g]
             nc.tensor.matmul_mx(
                 out=mu_sum[:],
                 lhsT=r_codes[:, gg, :].bitcast(FP8X4),
@@ -170,14 +181,21 @@ def tile_clusternet_pb_k_kernel(tc, x1, r, out_0, out_1):
                         )
                 banks_of[g].append(bank)
 
-        def empty(g):
-            xt_grouped_of[g] = stage.tile([P, PACK, P, PACK], BF16, align_bytes=64, name="xt_grouped")
-            xt_words = xt_grouped_of[g][:].bitcast(F32)
-            for b in range(PACK // 2):
-                nc.scalar.copy(
-                    out=xt_words[:, 2 * b : 2 * b + 2, :, :],
-                    in_=banks_of[g][b][:].rearrange("p j u m -> p j m u"),
+        def empty(g, b):
+            if b == 0:
+                xt_grouped_of[g] = stage.tile(
+                    [P, PACK, P, PACK], BF16, align_bytes=64, name="xt_grouped"
                 )
+            nc.scalar.copy(
+                out=xt_grouped_of[g][:].bitcast(F32)[:, 2 * b : 2 * b + 2, :, :],
+                in_=banks_of[g][b][:].rearrange("p j u m -> p j m u"),
+            )
+
+        def empty_first(g):
+            empty(g, 0)
+
+        def empty_second(g):
+            empty(g, 1)
 
         def quantise_features(g):
             nc.vector.quantize_mx(
@@ -186,19 +204,18 @@ def tile_clusternet_pb_k_kernel(tc, x1, r, out_0, out_1):
                 in_=xt_grouped_of[g][:].rearrange("p j m t -> p (j m t)"),
             )
 
+        inv_r_sum = const.tile([CENTROIDS, 1], F32)
+
         def centroids():
-            nc.scalar.activation(out=warm[:], in_=warm[:], func=ACT.Exp)
-            inv_r_sum = const.tile([CENTROIDS, 1], F32)
-            nc.vector.reciprocal(out=inv_r_sum[:], in_=r_sum[:, 0:1])
-            mu = const.tile([CENTROIDS, FEATURES], F32)
-            nc.vector.tensor_scalar_mul(out=mu[:], in0=mu_sum[:], scalar1=inv_r_sum[:])
-            nc.sync.dma_start(out=out_0, in_=mu[:])
             mu_bf = const.tile([CENTROIDS, FEATURES], BF16)
-            nc.vector.tensor_copy(out=mu_bf[:], in_=mu[:])
+            nc.vector.tensor_scalar_mul(out=mu_bf[:], in0=mu_sum[:], scalar1=inv_r_sum[:])
             mu_words = mu_bf[:].bitcast(F32)
             mu_bank = turned.tile([P, HALVES, CENTROIDS], F32, tag="bank")
             for u in range(HALVES):
                 nc.tensor.transpose(mu_bank[:, u, :], mu_words[:, u * P : (u + 1) * P], ident[:])
+            mu = const.tile([CENTROIDS, FEATURES], F32)
+            nc.vector.tensor_scalar_mul(out=mu[:], in0=mu_sum[:], scalar1=inv_r_sum[:])
+            nc.sync.dma_start(out=out_0, in_=mu[:])
             mu_grouped = const.tile([P, CENTROIDS, PACK], BF16, align_bytes=64)
             nc.vector.tensor_copy(
                 out=mu_grouped[:].bitcast(F32), in_=mu_bank[:].rearrange("p u c -> p c u")
@@ -223,11 +240,13 @@ def tile_clusternet_pb_k_kernel(tc, x1, r, out_0, out_1):
                     stop=True,
                 )
 
+        def find_top(g):
+            top_of[g] = stats.tile([P, PACK], F32, name="top")
+            nc.vector.tensor_reduce(out=top_of[g][:], in_=score_of[g][:], axis=AXIS.X, op=ALU.max)
+
         def find_shift(g):
-            top = stats.tile([P, PACK], F32)
-            nc.vector.tensor_reduce(out=top[:], in_=score_of[g][:], axis=AXIS.X, op=ALU.max)
             shift_of[g] = stats.tile([P, PACK], F32, name="shift")
-            nc.vector.tensor_scalar_mul(out=shift_of[g][:], in0=top[:], scalar1=-BETA)
+            nc.vector.tensor_scalar_mul(out=shift_of[g][:], in0=top_of[g][:], scalar1=-BETA)
 
         def exponentials(g):
             prob_of[g] = probs.tile([P, PACK, CENTROIDS], F32, name="prob")
@@ -242,12 +261,16 @@ def tile_clusternet_pb_k_kernel(tc, x1, r, out_0, out_1):
                     accum_out=total_of[g][:, j : j + 1],
                 )
 
+        def invert_total(g):
+            inv_total_of[g] = stats.tile([P, PACK], F32, name="inv_total")
+            nc.vector.reciprocal(out=inv_total_of[g][:], in_=total_of[g][:])
+
         def normalise(g):
-            inv_total = stats.tile([P, PACK], F32)
-            nc.vector.reciprocal(out=inv_total[:], in_=total_of[g][:])
             for j in range(PACK):
                 nc.vector.tensor_scalar_mul(
-                    out=prob_of[g][:, j, :], in0=prob_of[g][:, j, :], scalar1=inv_total[:, j : j + 1]
+                    out=prob_of[g][:, j, :],
+                    in0=prob_of[g][:, j, :],
+                    scalar1=inv_total_of[g][:, j : j + 1],
                 )
             nc.sync.dma_start(out=out_rows[g], in_=prob_of[g][:].rearrange("p j c -> p (j c)"))
 
@@ -257,23 +280,36 @@ def tile_clusternet_pb_k_kernel(tc, x1, r, out_0, out_1):
 
         for g in range(LOAD_AHEAD):
             load(g)
+        regroup_r(0)
         quantise_r(0)
-        first_score = PASSES + 1
-        for i in range(first_score + PASSES + 1):
+        mu_round = PASSES + 1
+        for i in range(mu_round + PASSES + 4):
             do(load, i + LOAD_AHEAD)
-            do(norms, i)
-            do(scale, i - 1)
+            do(squares_of, i)
+            do(sum_r, i)
             do(turn, i - TURN_LAG)
-            do(empty, i - TURN_LAG)
-            do(regroup, i - 1)
+            do(invert, i - 1)
             do(quantise_features, i - TURN_LAG - 1)
-            do(quantise_rows, i - 1)
-            do(row_pass, i - 1)
+            do(empty_first, i - TURN_LAG)
+            do(root, i)
+            do(empty_second, i - TURN_LAG)
+            do(scale, i - 1)
+            do(quantise_rows, i - 2)
+            do(row_pass, i - 2)
+            do(regroup, i - 1)
+            if (i + 2) % R_CHUNK == 0 and i + 2 < PASSES:
+                regroup_r((i + 2) // R_CHUNK)
             if (i + 1) % R_CHUNK == 0 and i + 1 < PASSES:
                 quantise_r((i + 1) // R_CHUNK)
             if i == PASSES:
+                nc.scalar.activation(out=warm[:], in_=warm[:], func=ACT.Exp)
+                nc.vector.reciprocal(out=inv_r_sum[:], in_=r_sum[:, 0:1])
+            if i == mu_round:
                 centroids()
-            do(score, i - first_score)
-            do(find_shift, i - first_score)
-            do(exponentials, i - first_score)
-            do(normalise, i - first_score - 1)
+            k = i - mu_round - 1
+            do(score, k)
+            do(find_top, k)
+            do(exponentials, k - 1)
+            do(normalise, k - 3)
+            do(find_shift, k)
+            do(invert_total, k - 2)

@@ -27,6 +27,7 @@ HALVES = 2
 ONES_COLS = 32
 
 LOAD_AHEAD = 4
+SCALAR_ROWS = 1
 TURN_LAG = 4
 
 FLOPS = 2 * 2 * ROWS * FEATURES * CENTROIDS
@@ -60,7 +61,7 @@ def tile_clusternet_pb_k_kernel(tc, x1, r, out_0, out_1):
         nc.vector.memset(ones[:], 1.0)
         warm = const.tile([P, 1], F32)
         nc.vector.memset(warm[:], 1.0)
-        nc.scalar.sqrt(out=warm[:], in_=warm[:])
+        nc.scalar.activation(out=warm[:], in_=warm[:], func=ACT.Abs_reciprocal_sqrt)
 
         xt_codes = keep.tile([P, PASSES, K_PASS], U32, align_bytes=64)
         xt_scales = keep.tile([P, PASSES, K_PASS], U8, align_bytes=64)
@@ -70,7 +71,7 @@ def tile_clusternet_pb_k_kernel(tc, x1, r, out_0, out_1):
         mu_sum = sums.tile([CENTROIDS, FEATURES], F32)
         r_sum = sums.tile([CENTROIDS, ONES_COLS], F32)
 
-        x_of, sum_sq_of, norm_of, inv_norm_of = {}, {}, {}, {}
+        x_of, sum_sq_of, inv_norm_of = {}, {}, {}
         x_grouped_of, x_codes_of, banks_of, xt_grouped_of = {}, {}, {}, {}
         r_of, r_grouped_of, r_codes_of = {}, {}, {}
         score_of, top_of, shift_of, prob_of, total_of, inv_total_of = {}, {}, {}, {}, {}, {}
@@ -113,13 +114,11 @@ def tile_clusternet_pb_k_kernel(tc, x1, r, out_0, out_1):
                     accum_out=sum_sq_of[g][:, j : j + 1],
                 )
 
-        def root(g):
-            norm_of[g] = stats.tile([P, PACK], F32, name="norm")
-            nc.scalar.sqrt(out=norm_of[g][:], in_=sum_sq_of[g][:])
-
-        def invert(g):
+        def inverse_root(g):
             inv_norm_of[g] = stats.tile([P, PACK], F32, name="inv_norm")
-            nc.vector.reciprocal(out=inv_norm_of[g][:], in_=norm_of[g][:])
+            nc.scalar.activation(
+                out=inv_norm_of[g][:], in_=sum_sq_of[g][:], func=ACT.Abs_reciprocal_sqrt
+            )
 
         def scale(g):
             for j in range(PACK):
@@ -267,11 +266,19 @@ def tile_clusternet_pb_k_kernel(tc, x1, r, out_0, out_1):
 
         def normalise(g):
             for j in range(PACK):
-                nc.vector.tensor_scalar_mul(
-                    out=prob_of[g][:, j, :],
-                    in0=prob_of[g][:, j, :],
-                    scalar1=inv_total_of[g][:, j : j + 1],
-                )
+                if j < SCALAR_ROWS:
+                    nc.scalar.activation(
+                        out=prob_of[g][:, j, :],
+                        in_=prob_of[g][:, j, :],
+                        func=ACT.Copy,
+                        scale=inv_total_of[g][:, j : j + 1],
+                    )
+                else:
+                    nc.vector.tensor_scalar_mul(
+                        out=prob_of[g][:, j, :],
+                        in0=prob_of[g][:, j, :],
+                        scalar1=inv_total_of[g][:, j : j + 1],
+                    )
             nc.sync.dma_start(out=out_rows[g], in_=prob_of[g][:].rearrange("p j c -> p (j c)"))
 
         def do(step, g):
@@ -288,10 +295,9 @@ def tile_clusternet_pb_k_kernel(tc, x1, r, out_0, out_1):
             do(squares_of, i)
             do(sum_r, i)
             do(turn, i - TURN_LAG)
-            do(invert, i - 1)
             do(quantise_features, i - TURN_LAG - 1)
             do(empty_first, i - TURN_LAG)
-            do(root, i)
+            do(inverse_root, i)
             do(empty_second, i - TURN_LAG)
             do(scale, i - 1)
             do(quantise_rows, i - 2)

@@ -27,6 +27,7 @@ HALVES = 2
 ONES_COLS = 32
 
 LOAD_AHEAD = 4
+RUN = 8
 SCALAR_ROWS = 1
 TURN_LAG = 4
 
@@ -89,8 +90,8 @@ def tile_clusternet_pb_k_kernel(tc, x1, r, out_0, out_1):
                 [P, R_CHUNK, CENTROIDS, PACK], BF16, align_bytes=64, name="r_grouped"
             )
             nc.vector.tensor_copy(
-                out=r_grouped_of[q][:].rearrange("p g (c i) j -> p g c j i", i=4),
-                in_=r_of[q][:].rearrange("p g j (c i) -> p g c j i", i=4),
+                out=r_grouped_of[q][:].rearrange("p g (c i) j -> p g c j i", i=RUN),
+                in_=r_of[q][:].rearrange("p g j (c i) -> p g c j i", i=RUN),
             )
 
         def quantise_r(q):
@@ -129,8 +130,8 @@ def tile_clusternet_pb_k_kernel(tc, x1, r, out_0, out_1):
         def regroup(g):
             x_grouped_of[g] = stage.tile([P, FEATURES, PACK], BF16, align_bytes=64, name="x_grouped")
             nc.vector.tensor_copy(
-                out=x_grouped_of[g][:].rearrange("p (f i) j -> p f j i", i=4),
-                in_=x_of[g][:].rearrange("p j (f i) -> p f j i", i=4),
+                out=x_grouped_of[g][:].rearrange("p (f i) j -> p f j i", i=RUN),
+                in_=x_of[g][:].rearrange("p j (f i) -> p f j i", i=RUN),
             )
 
         def quantise_rows(g):

@@ -28,8 +28,9 @@ ONES_COLS = 32
 
 LOAD_AHEAD = 4
 RUN = 8
-SCALAR_ROWS = 1
-TURN_LAG = 4
+FIRST_ON_VECTOR = (3,)
+TURN_LAG = 7
+XT_AHEAD = 7
 
 FLOPS = 2 * 2 * ROWS * FEATURES * CENTROIDS
 
@@ -45,15 +46,15 @@ def tile_clusternet_pb_k_kernel(tc, x1, r, out_0, out_1):
         const = ctx.enter_context(tc.tile_pool(name="const", bufs=1))
         keep = ctx.enter_context(tc.tile_pool(name="keep", bufs=1))
         x_pool = ctx.enter_context(tc.tile_pool(name="x", bufs=LOAD_AHEAD + TURN_LAG + 2))
-        r_pool = ctx.enter_context(tc.tile_pool(name="r", bufs=3))
+        r_pool = ctx.enter_context(tc.tile_pool(name="r", bufs=2))
         r_stage = ctx.enter_context(tc.tile_pool(name="r_stage", bufs=2))
-        scrap = ctx.enter_context(tc.tile_pool(name="scrap", bufs=4))
+        scrap = ctx.enter_context(tc.tile_pool(name="scrap", bufs=2))
         stage = ctx.enter_context(tc.tile_pool(name="stage", bufs=3))
+        xt_stage = ctx.enter_context(tc.tile_pool(name="xt_stage", bufs=XT_AHEAD))
         stats = ctx.enter_context(tc.tile_pool(name="stats", bufs=4))
-        probs = ctx.enter_context(tc.tile_pool(name="probs", bufs=6))
+        probs = ctx.enter_context(tc.tile_pool(name="probs", bufs=10))
         sums = ctx.enter_context(tc.psum_pool(name="sums", bufs=1))
-        turned = ctx.enter_context(tc.psum_pool(name="turned", bufs=3))
-        scores = ctx.enter_context(tc.psum_pool(name="scores", bufs=3))
+        banks = ctx.enter_context(tc.psum_pool(name="banks", bufs=6))
         ctx.enter_context(tc.manual_schedule())
 
         ident = const.tile([P, P], F32)
@@ -79,41 +80,53 @@ def tile_clusternet_pb_k_kernel(tc, x1, r, out_0, out_1):
 
         def load(g):
             x_of[g] = x_pool.tile([P, PACK, FEATURES], BF16, name="x_t")
-            nc.sync.dma_start(out=x_of[g][:], in_=x_rows[g])
-            if g % R_CHUNK == 0:
-                q = g // R_CHUNK
+            if g == 0:
+                for j in range(PACK):
+                    nc.sync.dma_start(out=x_of[g][:, j, :], in_=x_rows[g][:, j, :])
+            else:
+                nc.sync.dma_start(out=x_of[g][:], in_=x_rows[g])
+
+        def load_r(q, passes):
+            if passes.start == 0:
                 r_of[q] = r_pool.tile([P, R_CHUNK, PACK, CENTROIDS], BF16, name="r_t")
-                nc.sync.dma_start(out=r_of[q][:].rearrange("p g j c -> p g (j c)"), in_=r_rows[q])
-
-        def regroup_r(q):
-            r_grouped_of[q] = r_stage.tile(
-                [P, R_CHUNK, CENTROIDS, PACK], BF16, align_bytes=64, name="r_grouped"
+            nc.sync.dma_start(
+                out=r_of[q][:, passes].rearrange("p g j c -> p g (j c)"), in_=r_rows[q][:, passes, :]
             )
+
+        def regroup_r(q, passes):
+            if passes.start == 0:
+                r_grouped_of[q] = r_stage.tile(
+                    [P, R_CHUNK, CENTROIDS, PACK], BF16, align_bytes=64, name="r_grouped"
+                )
             nc.vector.tensor_copy(
-                out=r_grouped_of[q][:].rearrange("p g (c i) j -> p g c j i", i=RUN),
-                in_=r_of[q][:].rearrange("p g j (c i) -> p g c j i", i=RUN),
+                out=r_grouped_of[q][:, passes].rearrange("p g (c i) j -> p g c j i", i=RUN),
+                in_=r_of[q][:, passes].rearrange("p g j (c i) -> p g c j i", i=RUN),
             )
 
-        def quantise_r(q):
-            r_codes = r_stage.tile([P, R_CHUNK, CENTROIDS], U32, align_bytes=64)
-            r_scales = r_stage.tile([P, R_CHUNK, CENTROIDS], U8, align_bytes=64)
+        def quantise_r(q, passes):
+            if passes.start == 0:
+                r_codes = r_stage.tile([P, R_CHUNK, CENTROIDS], U32, align_bytes=64, name="r_codes")
+                r_scales = r_stage.tile([P, R_CHUNK, CENTROIDS], U8, align_bytes=64, name="r_scales")
+                r_codes_of[q] = (r_codes, r_scales)
+            r_codes, r_scales = r_codes_of[q]
             nc.vector.quantize_mx(
-                out=r_codes[:].rearrange("p g c -> p (g c)").bitcast(FP8X4),
-                scales=r_scales[:].rearrange("p g c -> p (g c)"),
-                in_=r_grouped_of[q][:].rearrange("p g c j -> p (g c j)"),
+                out=r_codes[:, passes].rearrange("p g c -> p (g c)").bitcast(FP8X4),
+                scales=r_scales[:, passes].rearrange("p g c -> p (g c)"),
+                in_=r_grouped_of[q][:, passes].rearrange("p g c j -> p (g c j)"),
             )
-            r_codes_of[q] = (r_codes, r_scales)
 
         def squares_of(g):
             sum_sq_of[g] = stats.tile([P, PACK], F32, name="sum_sq")
             for j in range(PACK):
-                squares = scrap.tile([P, FEATURES], BF16)
-                nc.scalar.activation(
-                    out=squares[:],
-                    in_=x_of[g][:, j, :],
-                    func=ACT.Square,
-                    accum_out=sum_sq_of[g][:, j : j + 1],
-                )
+                row, sum_sq = x_of[g][:, j, :], sum_sq_of[g][:, j : j + 1]
+                if g == 0 and j in FIRST_ON_VECTOR:
+                    squares = scrap.tile([P, FEATURES], BF16, tag="vector", name="squares")
+                    nc.vector.scalar_tensor_tensor(
+                        out=squares[:], in0=row, scalar=1.0, in1=row, op0=ALU.mult, op1=ALU.mult, accum_out=sum_sq
+                    )
+                else:
+                    squares = scrap.tile([P, FEATURES], BF16, tag="scalar", name="squares")
+                    nc.scalar.activation(out=squares[:], in_=row, func=ACT.Square, accum_out=sum_sq)
 
         def inverse_root(g):
             inv_norm_of[g] = stats.tile([P, PACK], F32, name="inv_norm")
@@ -173,7 +186,7 @@ def tile_clusternet_pb_k_kernel(tc, x1, r, out_0, out_1):
             x_words = x_of[g][:].bitcast(F32)
             banks_of[g] = []
             for b in range(PACK // 2):
-                bank = turned.tile([P, 2, HALVES, P], F32)
+                bank = banks.tile([P, 2, HALVES, P], F32, tag="bank", name="bank")
                 for jj in range(2):
                     for u in range(HALVES):
                         nc.tensor.transpose(
@@ -183,7 +196,7 @@ def tile_clusternet_pb_k_kernel(tc, x1, r, out_0, out_1):
 
         def empty(g, b):
             if b == 0:
-                xt_grouped_of[g] = stage.tile(
+                xt_grouped_of[g] = xt_stage.tile(
                     [P, PACK, P, PACK], BF16, align_bytes=64, name="xt_grouped"
                 )
             nc.scalar.copy(
@@ -206,28 +219,39 @@ def tile_clusternet_pb_k_kernel(tc, x1, r, out_0, out_1):
 
         inv_r_sum = const.tile([CENTROIDS, 1], F32)
 
-        def centroids():
-            mu_bf = const.tile([CENTROIDS, FEATURES], BF16)
+        mu_bf = const.tile([CENTROIDS, FEATURES], BF16)
+        mu = const.tile([CENTROIDS, FEATURES], F32)
+        mu_grouped = const.tile([P, CENTROIDS, PACK], BF16, align_bytes=64)
+        mu_banks = []
+
+        def divide():
             nc.vector.tensor_scalar_mul(out=mu_bf[:], in0=mu_sum[:], scalar1=inv_r_sum[:])
+
+        def turn_mu():
             mu_words = mu_bf[:].bitcast(F32)
-            mu_bank = turned.tile([P, HALVES, CENTROIDS], F32, tag="bank")
+            mu_bank = banks.tile([P, HALVES, CENTROIDS], F32, tag="bank", name="mu_bank")
             for u in range(HALVES):
                 nc.tensor.transpose(mu_bank[:, u, :], mu_words[:, u * P : (u + 1) * P], ident[:])
-            mu = const.tile([CENTROIDS, FEATURES], F32)
-            nc.vector.tensor_scalar_mul(out=mu[:], in0=mu_sum[:], scalar1=inv_r_sum[:])
-            nc.sync.dma_start(out=out_0, in_=mu[:])
-            mu_grouped = const.tile([P, CENTROIDS, PACK], BF16, align_bytes=64)
+            mu_banks.append(mu_bank)
+
+        def empty_mu():
             nc.vector.tensor_copy(
-                out=mu_grouped[:].bitcast(F32), in_=mu_bank[:].rearrange("p u c -> p c u")
+                out=mu_grouped[:].bitcast(F32), in_=mu_banks[0][:].rearrange("p u c -> p c u")
             )
+
+        def quantise_mu():
             nc.vector.quantize_mx(
                 out=mu_codes[:].bitcast(FP8X4),
                 scales=mu_scales[:],
                 in_=mu_grouped[:].rearrange("p c t -> p (c t)"),
             )
 
+        def store_mu():
+            nc.scalar.activation(out=mu[:], in_=mu_sum[:], func=ACT.Copy, scale=inv_r_sum[:])
+            nc.sync.dma_start(out=out_0, in_=mu[:])
+
         def score(g):
-            score_of[g] = scores.tile([P, PACK, CENTROIDS], F32, name="score")
+            score_of[g] = banks.tile([P, PACK, CENTROIDS], F32, tag="bank", name="score")
             for j in range(PACK):
                 cols = slice(j * P, (j + 1) * P)
                 nc.tensor.matmul_mx(
@@ -265,9 +289,12 @@ def tile_clusternet_pb_k_kernel(tc, x1, r, out_0, out_1):
             inv_total_of[g] = stats.tile([P, PACK], F32, name="inv_total")
             nc.vector.reciprocal(out=inv_total_of[g][:], in_=total_of[g][:])
 
+        def scalar_rows(g):
+            return 2 if g < TURN_LAG - 1 or g == PASSES - 1 else 1
+
         def normalise(g):
             for j in range(PACK):
-                if j < SCALAR_ROWS:
+                if j < scalar_rows(g):
                     nc.scalar.activation(
                         out=prob_of[g][:, j, :],
                         in_=prob_of[g][:, j, :],
@@ -280,23 +307,36 @@ def tile_clusternet_pb_k_kernel(tc, x1, r, out_0, out_1):
                         in0=prob_of[g][:, j, :],
                         scalar1=inv_total_of[g][:, j : j + 1],
                     )
-            nc.sync.dma_start(out=out_rows[g], in_=prob_of[g][:].rearrange("p j c -> p (j c)"))
+            if g < PASSES - 1:
+                nc.sync.dma_start(out=out_rows[g], in_=prob_of[g][:].rearrange("p j c -> p (j c)"))
+            else:
+                for half in (slice(0, 2), slice(2, PACK)):
+                    nc.sync.dma_start(
+                        out=out_rows[g].rearrange("p (j c) -> p j c", j=PACK)[:, half, :],
+                        in_=prob_of[g][:, half, :],
+                    )
 
         def do(step, g):
             if 0 <= g < PASSES:
                 step(g)
 
-        for g in range(LOAD_AHEAD):
+        halves = [slice(0, R_CHUNK // 2), slice(R_CHUNK // 2, R_CHUNK)]
+        whole = slice(0, R_CHUNK)
+        load_r(0, halves[0])
+        load(0)
+        load_r(0, halves[1])
+        for g in range(1, LOAD_AHEAD):
             load(g)
-        regroup_r(0)
-        quantise_r(0)
-        mu_round = PASSES + 1
-        for i in range(mu_round + PASSES + 4):
+        regroup_r(0, halves[0])
+        quantise_r(0, halves[0])
+        for i in range(PASSES):
             do(load, i + LOAD_AHEAD)
+            if i % R_CHUNK == 0 and i + R_CHUNK < PASSES:
+                load_r(i // R_CHUNK + 1, whole)
             do(squares_of, i)
             do(sum_r, i)
             do(turn, i - TURN_LAG)
-            do(quantise_features, i - TURN_LAG - 1)
+            do(quantise_features, i - TURN_LAG - 2)
             do(empty_first, i - TURN_LAG)
             do(inverse_root, i)
             do(empty_second, i - TURN_LAG)
@@ -304,19 +344,55 @@ def tile_clusternet_pb_k_kernel(tc, x1, r, out_0, out_1):
             do(quantise_rows, i - 2)
             do(row_pass, i - 2)
             do(regroup, i - 1)
-            if (i + 2) % R_CHUNK == 0 and i + 2 < PASSES:
-                regroup_r((i + 2) // R_CHUNK)
-            if (i + 1) % R_CHUNK == 0 and i + 1 < PASSES:
-                quantise_r((i + 1) // R_CHUNK)
-            if i == PASSES:
-                nc.scalar.activation(out=warm[:], in_=warm[:], func=ACT.Exp)
-                nc.vector.reciprocal(out=inv_r_sum[:], in_=r_sum[:, 0:1])
-            if i == mu_round:
-                centroids()
-            k = i - mu_round - 1
+            if i == 0:
+                regroup_r(0, halves[1])
+                quantise_r(0, halves[1])
+            if (i + 2) % R_CHUNK == 0 and R_CHUNK <= i + 2 < PASSES:
+                regroup_r((i + 2) // R_CHUNK, whole)
+            if (i + 1) % R_CHUNK == 0 and R_CHUNK <= i + 1 < PASSES:
+                quantise_r((i + 1) // R_CHUNK, whole)
+
+        late_turns = list(range(PASSES - TURN_LAG, PASSES))
+        late_quantises = list(range(PASSES - TURN_LAG - 2, PASSES))
+
+        def turn_late(n):
+            for g in late_turns[:n]:
+                turn(g)
+                empty_first(g)
+                empty_second(g)
+                late_turns.remove(g)
+
+        def quantise_late():
+            for g in late_quantises[:1]:
+                quantise_features(g)
+                late_quantises.remove(g)
+
+        nc.scalar.activation(out=warm[:], in_=warm[:], func=ACT.Exp)
+        scale(PASSES - 1)
+        turn_late(2)
+        quantise_rows(PASSES - 2)
+        row_pass(PASSES - 2)
+        regroup(PASSES - 1)
+        turn_late(2)
+        nc.vector.reciprocal(out=inv_r_sum[:], in_=r_sum[:, 0:1])
+        quantise_late()
+        quantise_rows(PASSES - 1)
+        row_pass(PASSES - 1)
+        turn_late(2)
+        quantise_late()
+        divide()
+        turn_mu()
+        turn_late(TURN_LAG)
+        quantise_late()
+        empty_mu()
+        quantise_late()
+        quantise_mu()
+        store_mu()
+        for k in range(PASSES + 4):
             do(score, k)
             do(find_top, k)
             do(exponentials, k - 1)
             do(normalise, k - 3)
             do(find_shift, k)
             do(invert_total, k - 2)
+            quantise_late()

@@ -270,7 +270,7 @@ def tile_clusternet_pb_k_kernel(tc, x1, r, out_0, out_1):
 
         def find_shift(g):
             shift_of[g] = stats.tile([P, PACK], F32, name="shift")
-            nc.vector.tensor_scalar_mul(out=shift_of[g][:], in0=top_of[g][:], scalar1=-BETA)
+            nc.scalar.mul(shift_of[g][:], top_of[g][:], -BETA)
 
         def exponentials(g):
             prob_of[g] = probs.tile([P, PACK, CENTROIDS], F32, name="prob")
@@ -290,7 +290,7 @@ def tile_clusternet_pb_k_kernel(tc, x1, r, out_0, out_1):
             nc.vector.reciprocal(out=inv_total_of[g][:], in_=total_of[g][:])
 
         def scalar_rows(g):
-            return 2 if g < TURN_LAG - 1 or g == PASSES - 1 else 1
+            return 2 if g < TURN_LAG - 1 or g == PASSES - 1 else g % 2
 
         def normalise(g):
             for j in range(PACK):
@@ -367,7 +367,6 @@ def tile_clusternet_pb_k_kernel(tc, x1, r, out_0, out_1):
                 quantise_features(g)
                 late_quantises.remove(g)
 
-        nc.scalar.activation(out=warm[:], in_=warm[:], func=ACT.Exp)
         scale(PASSES - 1)
         turn_late(2)
         quantise_rows(PASSES - 2)
@@ -387,12 +386,14 @@ def tile_clusternet_pb_k_kernel(tc, x1, r, out_0, out_1):
         empty_mu()
         quantise_late()
         quantise_mu()
+        quantise_late()
+        nc.scalar.activation(out=warm[:], in_=warm[:], func=ACT.Exp)
         store_mu()
-        for k in range(PASSES + 4):
+        for k in range(PASSES + 5):
             do(score, k)
             do(find_top, k)
-            do(exponentials, k - 1)
-            do(normalise, k - 3)
-            do(find_shift, k)
-            do(invert_total, k - 2)
+            do(find_shift, k - 1)
+            do(exponentials, k - 2)
+            do(normalise, k - 4)
+            do(invert_total, k - 3)
             quantise_late()

@@ -27,7 +27,7 @@ HALVES = 2
 ONES_COLS = 32
 
 LOAD_AHEAD = 4
-RUN = 8
+RUN = 2
 FIRST_ON_VECTOR = (3,)
 TURN_LAG = 7
 XT_AHEAD = 7
@@ -290,7 +290,7 @@ def tile_clusternet_pb_k_kernel(tc, x1, r, out_0, out_1):
             nc.vector.reciprocal(out=inv_total_of[g][:], in_=total_of[g][:])
 
         def scalar_rows(g):
-            return 2 if g < TURN_LAG - 1 or g == PASSES - 1 else g % 2
+            return 2 if g < TURN_LAG - 1 or g == PASSES - 1 else g % 2 if g < PASSES - 4 else 0
 
         def normalise(g):
             for j in range(PACK):

from contextlib import ExitStack

import concourse.mybir as mybir
from concourse.masks import make_identity

F32 = mybir.dt.float32
BF16 = mybir.dt.bfloat16
U32 = mybir.dt.uint32
U8 = mybir.dt.uint8
FP8X4 = mybir.dt.float8_e4m3fn_x4
ACT = mybir.ActivationFunctionType
ALU = mybir.AluOpType
AXIS = mybir.AxisListType

P = 128
PACK = 4
K_PASS = P * PACK

ROWS = 16384
FEATURES = 512
CENTROIDS = 128
BETA = 5.0

PASSES = ROWS // K_PASS
R_CHUNK = 4
HALVES = 2
ONES_COLS = 32

LOAD_AHEAD = 4
RUN = 2
FIRST_ON_VECTOR = (3,)
TURN_LAG = 7
XT_AHEAD = 7

FLOPS = 2 * 2 * ROWS * FEATURES * CENTROIDS


def tile_clusternet_pb_k_kernel(tc, x1, r, out_0, out_1):
    nc = tc.nc

    x_rows = x1.rearrange("(g p j) f -> g p j f", p=P, j=PACK)
    r_rows = r.rearrange("(q g p j) c -> q p g (j c)", g=R_CHUNK, p=P, j=PACK)
    out_rows = out_1.rearrange("(g p j) c -> g p (j c)", p=P, j=PACK)

    with ExitStack() as ctx:
        const = ctx.enter_context(tc.tile_pool(name="const", bufs=1))
        keep = ctx.enter_context(tc.tile_pool(name="keep", bufs=1))
        x_pool = ctx.enter_context(tc.tile_pool(name="x", bufs=LOAD_AHEAD + TURN_LAG + 2))
        r_pool = ctx.enter_context(tc.tile_pool(name="r", bufs=2))
        r_stage = ctx.enter_context(tc.tile_pool(name="r_stage", bufs=2))
        scrap = ctx.enter_context(tc.tile_pool(name="scrap", bufs=2))
        stage = ctx.enter_context(tc.tile_pool(name="stage", bufs=3))
        xt_stage = ctx.enter_context(tc.tile_pool(name="xt_stage", bufs=XT_AHEAD))
        stats = ctx.enter_context(tc.tile_pool(name="stats", bufs=4))
        probs = ctx.enter_context(tc.tile_pool(name="probs", bufs=10))
        sums = ctx.enter_context(tc.psum_pool(name="sums", bufs=1))
        banks = ctx.enter_context(tc.psum_pool(name="banks", bufs=6))
        ctx.enter_context(tc.manual_schedule())

        ident = const.tile([P, P], F32)
        make_identity(nc, ident[:])
        ones = const.tile([P, ONES_COLS], BF16)
        nc.vector.memset(ones[:], 1.0)
        warm = const.tile([P, 1], F32)
        nc.vector.memset(warm[:], 1.0)
        nc.scalar.activation(out=warm[:], in_=warm[:], func=ACT.Abs_reciprocal_sqrt)

        xt_codes = keep.tile([P, PASSES, K_PASS], U32, align_bytes=64)
        xt_scales = keep.tile([P, PASSES, K_PASS], U8, align_bytes=64)
        mu_codes = keep.tile([P, CENTROIDS], U32, align_bytes=64)
        mu_scales = keep.tile([P, CENTROIDS], U8, align_bytes=64)

        mu_sum = sums.tile([CENTROIDS, FEATURES], F32)
        r_sum = sums.tile([CENTROIDS, ONES_COLS], F32)

        x_of, sum_sq_of, inv_norm_of = {}, {}, {}
        x_grouped_of, x_codes_of, banks_of, xt_grouped_of = {}, {}, {}, {}
        r_of, r_grouped_of, r_codes_of = {}, {}, {}
        score_of, top_of, shift_of, prob_of, total_of, inv_total_of = {}, {}, {}, {}, {}, {}

        def load(g):
            x_of[g] = x_pool.tile([P, PACK, FEATURES], BF16, name="x_t")
            if g == 0:
                for j in range(PACK):
                    nc.sync.dma_start(out=x_of[g][:, j, :], in_=x_rows[g][:, j, :])
            else:
                nc.sync.dma_start(out=x_of[g][:], in_=x_rows[g])

        def load_r(q, passes):
            if passes.start == 0:
                r_of[q] = r_pool.tile([P, R_CHUNK, PACK, CENTROIDS], BF16, name="r_t")
            nc.sync.dma_start(
                out=r_of[q][:, passes].rearrange("p g j c -> p g (j c)"), in_=r_rows[q][:, passes, :]
            )

        def regroup_r(q, passes):
            if passes.start == 0:
                r_grouped_of[q] = r_stage.tile(
                    [P, R_CHUNK, CENTROIDS, PACK], BF16, align_bytes=64, name="r_grouped"
                )
            nc.vector.tensor_copy(
                out=r_grouped_of[q][:, passes].rearrange("p g (c i) j -> p g c j i", i=RUN),
                in_=r_of[q][:, passes].rearrange("p g j (c i) -> p g c j i", i=RUN),
            )

        def quantise_r(q, passes):
            if passes.start == 0:
                r_codes = r_stage.tile([P, R_CHUNK, CENTROIDS], U32, align_bytes=64, name="r_codes")
                r_scales = r_stage.tile([P, R_CHUNK, CENTROIDS], U8, align_bytes=64, name="r_scales")
                r_codes_of[q] = (r_codes, r_scales)
            r_codes, r_scales = r_codes_of[q]
            nc.vector.quantize_mx(
                out=r_codes[:, passes].rearrange("p g c -> p (g c)").bitcast(FP8X4),
                scales=r_scales[:, passes].rearrange("p g c -> p (g c)"),
                in_=r_grouped_of[q][:, passes].rearrange("p g c j -> p (g c j)"),
            )

        def squares_of(g):
            sum_sq_of[g] = stats.tile([P, PACK], F32, name="sum_sq")
            for j in range(PACK):
                row, sum_sq = x_of[g][:, j, :], sum_sq_of[g][:, j : j + 1]
                if g == 0 and j in FIRST_ON_VECTOR:
                    squares = scrap.tile([P, FEATURES], BF16, tag="vector", name="squares")
                    nc.vector.scalar_tensor_tensor(
                        out=squares[:], in0=row, scalar=1.0, in1=row, op0=ALU.mult, op1=ALU.mult, accum_out=sum_sq
                    )
                else:
                    squares = scrap.tile([P, FEATURES], BF16, tag="scalar", name="squares")
                    nc.scalar.activation(out=squares[:], in_=row, func=ACT.Square, accum_out=sum_sq)

        def inverse_root(g):
            inv_norm_of[g] = stats.tile([P, PACK], F32, name="inv_norm")
            nc.scalar.activation(
                out=inv_norm_of[g][:], in_=sum_sq_of[g][:], func=ACT.Abs_reciprocal_sqrt
            )

        def scale(g):
            for j in range(PACK):
                nc.vector.tensor_scalar_mul(
                    out=x_of[g][:, j, :], in0=x_of[g][:, j, :], scalar1=inv_norm_of[g][:, j : j + 1]
                )

        def regroup(g):
            x_grouped_of[g] = stage.tile([P, FEATURES, PACK], BF16, align_bytes=64, name="x_grouped")
            nc.vector.tensor_copy(
                out=x_grouped_of[g][:].rearrange("p (f i) j -> p f j i", i=RUN),
                in_=x_of[g][:].rearrange("p j (f i) -> p f j i", i=RUN),
            )

        def quantise_rows(g):
            x_codes = stage.tile([P, FEATURES], U32, align_bytes=64)
            x_scales = stage.tile([P, FEATURES], U8, align_bytes=64)
            nc.vector.quantize_mx(
                out=x_codes[:].bitcast(FP8X4),
                scales=x_scales[:],
                in_=x_grouped_of[g][:].rearrange("p f j -> p (f j)"),
            )
            x_codes_of[g] = (x_codes, x_scales)

        def sum_r(g):
            q, gg = divmod(g, R_CHUNK)
            for j in range(PACK):
                nc.tensor.matmul(
                    out=r_sum[:],
                    lhsT=r_of[q][:, gg, j, :],
                    rhs=ones[:],
                    start=(g == 0 and j == 0),
                    stop=(g == PASSES - 1 and j == PACK - 1),
                )

        def row_pass(g):
            q, gg = divmod(g, R_CHUNK)
            r_codes, r_scales = r_codes_of[q]
            x_codes, x_scales = x_codes_of[g]
            nc.tensor.matmul_mx(
                out=mu_sum[:],
                lhsT=r_codes[:, gg, :].bitcast(FP8X4),
                lhsT_scale=r_scales[:, gg, :],
                rhs=x_codes[:].bitcast(FP8X4),
                rhs_scale=x_scales[:],
                start=(g == 0),
                stop=(g == PASSES - 1),
            )

        def turn(g):
            x_words = x_of[g][:].bitcast(F32)
            banks_of[g] = []
            for b in range(PACK // 2):
                bank = banks.tile([P, 2, HALVES, P], F32, tag="bank", name="bank")
                for jj in range(2):
                    for u in range(HALVES):
                        nc.tensor.transpose(
                            bank[:, jj, u, :], x_words[:, 2 * b + jj, u * P : (u + 1) * P], ident[:]
                        )
                banks_of[g].append(bank)

        def empty(g, b):
            if b == 0:
                xt_grouped_of[g] = xt_stage.tile(
                    [P, PACK, P, PACK], BF16, align_bytes=64, name="xt_grouped"
                )
            nc.scalar.copy(
                out=xt_grouped_of[g][:].bitcast(F32)[:, 2 * b : 2 * b + 2, :, :],
                in_=banks_of[g][b][:].rearrange("p j u m -> p j m u"),
            )

        def empty_first(g):
            empty(g, 0)

        def empty_second(g):
            empty(g, 1)

        def quantise_features(g):
            nc.vector.quantize_mx(
                out=xt_codes[:, g, :].bitcast(FP8X4),
                scales=xt_scales[:, g, :],
                in_=xt_grouped_of[g][:].rearrange("p j m t -> p (j m t)"),
            )

        inv_r_sum = const.tile([CENTROIDS, 1], F32)

        mu_bf = const.tile([CENTROIDS, FEATURES], BF16)
        mu = const.tile([CENTROIDS, FEATURES], F32)
        mu_grouped = const.tile([P, CENTROIDS, PACK], BF16, align_bytes=64)
        mu_banks = []

        def divide():
            nc.vector.tensor_scalar_mul(out=mu_bf[:], in0=mu_sum[:], scalar1=inv_r_sum[:])

        def turn_mu():
            mu_words = mu_bf[:].bitcast(F32)
            mu_bank = banks.tile([P, HALVES, CENTROIDS], F32, tag="bank", name="mu_bank")
            for u in range(HALVES):
                nc.tensor.transpose(mu_bank[:, u, :], mu_words[:, u * P : (u + 1) * P], ident[:])
            mu_banks.append(mu_bank)

        def empty_mu():
            nc.vector.tensor_copy(
                out=mu_grouped[:].bitcast(F32), in_=mu_banks[0][:].rearrange("p u c -> p c u")
            )

        def quantise_mu():
            nc.vector.quantize_mx(
                out=mu_codes[:].bitcast(FP8X4),
                scales=mu_scales[:],
                in_=mu_grouped[:].rearrange("p c t -> p (c t)"),
            )

        def store_mu():
            nc.scalar.activation(out=mu[:], in_=mu_sum[:], func=ACT.Copy, scale=inv_r_sum[:])
            nc.sync.dma_start(out=out_0, in_=mu[:])

        def score(g):
            score_of[g] = banks.tile([P, PACK, CENTROIDS], F32, tag="bank", name="score")
            for j in range(PACK):
                cols = slice(j * P, (j + 1) * P)
                nc.tensor.matmul_mx(
                    out=score_of[g][:, j, :],
                    lhsT=xt_codes[:, g, cols].bitcast(FP8X4),
                    lhsT_scale=xt_scales[:, g, cols],
                    rhs=mu_codes[:].bitcast(FP8X4),
                    rhs_scale=mu_scales[:],
                    start=True,
                    stop=True,
                )

        def find_top(g):
            top_of[g] = stats.tile([P, PACK], F32, name="top")
            nc.vector.tensor_reduce(out=top_of[g][:], in_=score_of[g][:], axis=AXIS.X, op=ALU.max)

        def find_shift(g):
            shift_of[g] = stats.tile([P, PACK], F32, name="shift")
            nc.scalar.mul(shift_of[g][:], top_of[g][:], -BETA)

        def exponentials(g):
            prob_of[g] = probs.tile([P, PACK, CENTROIDS], F32, name="prob")
            total_of[g] = stats.tile([P, PACK], F32, name="total")
            for j in range(PACK):
                nc.scalar.activation(
                    out=prob_of[g][:, j, :],
                    in_=score_of[g][:, j, :],
                    func=ACT.Exp,
                    bias=shift_of[g][:, j : j + 1],
                    scale=BETA,
                    accum_out=total_of[g][:, j : j + 1],
                )

        def invert_total(g):
            inv_total_of[g] = stats.tile([P, PACK], F32, name="inv_total")
            nc.vector.reciprocal(out=inv_total_of[g][:], in_=total_of[g][:])

        def scalar_rows(g):
            return 2 if g < TURN_LAG - 1 or g == PASSES - 1 else g % 2 if g < PASSES - 4 else 0

        def normalise(g):
            for j in range(PACK):
                if j < scalar_rows(g):
                    nc.scalar.activation(
                        out=prob_of[g][:, j, :],
                        in_=prob_of[g][:, j, :],
                        func=ACT.Copy,
                        scale=inv_total_of[g][:, j : j + 1],
                    )
                else:
                    nc.vector.tensor_scalar_mul(
                        out=prob_of[g][:, j, :],
                        in0=prob_of[g][:, j, :],
                        scalar1=inv_total_of[g][:, j : j + 1],
                    )
            if g < PASSES - 1:
                nc.sync.dma_start(out=out_rows[g], in_=prob_of[g][:].rearrange("p j c -> p (j c)"))
            else:
                for half in (slice(0, 2), slice(2, PACK)):
                    nc.sync.dma_start(
                        out=out_rows[g].rearrange("p (j c) -> p j c", j=PACK)[:, half, :],
                        in_=prob_of[g][:, half, :],
                    )

        def do(step, g):
            if 0 <= g < PASSES:
                step(g)

        halves = [slice(0, R_CHUNK // 2), slice(R_CHUNK // 2, R_CHUNK)]
        whole = slice(0, R_CHUNK)
        load_r(0, halves[0])
        load(0)
        load_r(0, halves[1])
        for g in range(1, LOAD_AHEAD):
            load(g)
        regroup_r(0, halves[0])
        quantise_r(0, halves[0])
        for i in range(PASSES):
            do(load, i + LOAD_AHEAD)
            if i % R_CHUNK == 0 and i + R_CHUNK < PASSES:
                load_r(i // R_CHUNK + 1, whole)
            do(squares_of, i)
            do(sum_r, i)
            do(turn, i - TURN_LAG)
            do(quantise_features, i - TURN_LAG - 2)
            do(empty_first, i - TURN_LAG)
            do(inverse_root, i)
            do(empty_second, i - TURN_LAG)
            do(scale, i - 1)
            do(quantise_rows, i - 2)
            do(row_pass, i - 2)
            do(regroup, i - 1)
            if i == 0:
                regroup_r(0, halves[1])
                quantise_r(0, halves[1])
            if (i + 2) % R_CHUNK == 0 and R_CHUNK <= i + 2 < PASSES:
                regroup_r((i + 2) // R_CHUNK, whole)
            if (i + 1) % R_CHUNK == 0 and R_CHUNK <= i + 1 < PASSES:
                quantise_r((i + 1) // R_CHUNK, whole)

        late_turns = list(range(PASSES - TURN_LAG, PASSES))
        late_quantises = list(range(PASSES - TURN_LAG - 2, PASSES))

        def turn_late(n):
            for g in late_turns[:n]:
                turn(g)
                empty_first(g)
                empty_second(g)
                late_turns.remove(g)

        def quantise_late():
            for g in late_quantises[:1]:
                quantise_features(g)
                late_quantises.remove(g)

        scale(PASSES - 1)
        turn_late(2)
        quantise_rows(PASSES - 2)
        row_pass(PASSES - 2)
        regroup(PASSES - 1)
        turn_late(2)
        nc.vector.reciprocal(out=inv_r_sum[:], in_=r_sum[:, 0:1])
        quantise_late()
        quantise_rows(PASSES - 1)
        row_pass(PASSES - 1)
        turn_late(2)
        quantise_late()
        divide()
        turn_mu()
        turn_late(TURN_LAG)
        quantise_late()
        empty_mu()
        quantise_late()
        quantise_mu()
        quantise_late()
        nc.scalar.activation(out=warm[:], in_=warm[:], func=ACT.Exp)
        store_mu()
        for k in range(PASSES + 5):
            do(score, k)
            do(find_top, k)
            do(find_shift, k - 1)
            do(exponentials, k - 2)
            do(normalise, k - 4)
            do(invert_total, k - 3)
            quantise_late()
